import numpy as np
import ml_dtypes


def mxq(x, axis, fmt="e4m3"):
    dtype, down = {"e4m3": (ml_dtypes.float8_e4m3fn, 7), "e5m2": (ml_dtypes.float8_e5m2, 14)}[fmt]
    v = np.moveaxis(np.asarray(x, np.float32).astype(ml_dtypes.bfloat16).astype(np.float64), axis, -1)
    blocks = v.reshape(v.shape[:-1] + (-1, 32))
    amax = np.abs(blocks).max(-1, keepdims=True)
    byte = np.maximum(np.where(amax > 0, np.frexp(amax)[1] - 1 + 127, 0) - down, 1)
    scale = np.exp2(byte - 127.0)
    codes = (blocks / scale).astype(np.float32).astype(dtype).astype(np.float64)
    return np.moveaxis((codes * scale).reshape(v.shape), -1, axis)


WIDE = False


def mx_kscale(k):
    if not WIDE:
        return np.ones(k)
    levels = np.array([10, -10, 5, -5, 0])
    a = np.random.permutation(np.resize(levels, k // 512 * 4)).reshape(k // 512, 4)
    idx = np.arange(k)
    return np.exp2(a[idx // 512, idx % 128 // 32])


BF16 = ml_dtypes.bfloat16


def bf(x):
    return np.asarray(x, np.float32).astype(BF16)


def f64(x):
    return np.asarray(x).astype(np.float64)


D, KW, STRIDE, STACK, B, O = 64, 19, 3, 4, 256, 128
W_IN = D * D
POS = (D - KW) // STRIDE + 1
K = STACK * POS * POS


def build_mask():
    base_new = np.tile(np.arange(KW), KW)
    addition_new = np.repeat(np.arange(KW) * D, KW)
    index_1 = addition_new + base_new
    index_width = np.tile(index_1, POS)
    addition_width = np.repeat(STRIDE * np.arange(POS), KW * KW)
    index_row = index_width + addition_width
    index_column = np.tile(index_row, POS)
    addition_height = np.repeat(STRIDE * D * np.arange(POS), KW * KW * POS)
    index_final = index_column + addition_height
    stack = np.repeat(np.arange(POS * POS), KW * KW)
    block = np.zeros((POS * POS, W_IN))
    block[stack, index_final] = 1.0
    return np.vstack([block] * STACK)


def setup_inputs():
    s = mx_kscale(W_IN)
    return {"z": bf(np.random.standard_normal((B, W_IN)) * s),
            "T1": bf(np.random.standard_normal((K, W_IN)) * 0.7 / np.sqrt(KW * KW) / s),
            "T2": bf(np.random.standard_normal((K, W_IN)) * 0.7 / np.sqrt(KW * KW) / s),
            "T0": bf(np.random.standard_normal(K)),
            "mask": bf(build_mask())}


def reference(z, T1, T2, T0, mask):
    zq = mxq(f64(z).reshape(-1, D * D), 1, "e4m3")
    m = f64(mask)
    x1 = zq @ mxq(m * f64(T1), 1, "e4m3").T
    x2 = 2.0 * (zq @ mxq(m * f64(T2), 1, "e4m3").T) * x1 - f64(T0)
    return x1, x2

@@ -1,0 +1,221 @@
+import contextlib
+
+import concourse.mybir as mybir
+from concourse.masks import make_identity
+
+F32 = mybir.dt.float32
+BF16 = mybir.dt.bfloat16
+U32 = mybir.dt.uint32
+U8 = mybir.dt.uint8
+FP8X4 = mybir.dt.float8_e4m3fn_x4
+MULT = mybir.AluOpType.mult
+SUBTRACT = mybir.AluOpType.subtract
+
+P = 128
+IMG = 64
+PATCH = 19
+STRIDE = 3
+POS = 16
+STACK = 4
+BATCH = 256
+K = IMG * IMG
+ROWS = STACK * POS * POS
+M_TILES = BATCH // P
+
+PY_PER_GROUP = 2
+GROUPS = POS // PY_PER_GROUP
+J = PY_PER_GROUP * POS
+WIN_Y = STRIDE * (PY_PER_GROUP - 1) + PATCH
+WIN = WIN_Y * IMG
+CHUNK = 256
+CHUNK_Y = CHUNK // IMG
+CHUNKS = 6
+K_PASS = 512
+PASSES = K // K_PASS
+
+FLOPS = 2 * 2 * BATCH * ROWS * PATCH * PATCH
+BYTES = 2 * BATCH * K + 3 * 2 * ROWS * PATCH * PATCH + 2 * ROWS + 2 * 4 * BATCH * ROWS
+
+
+def group_geometry(g):
+    y0 = STRIDE * PY_PER_GROUP * g
+    chunk0 = y0 // CHUNK_Y
+    margin = (y0 % CHUNK_Y) * IMG
+    first_pass = chunk0 // 2
+    last_pass = (chunk0 + CHUNKS - 1) // 2
+    return y0, chunk0, margin, first_pass, last_pass
+
+
+def tile_chebyshev_l3_sparsed32_stack_pa_kernel(tc, z, T1, T2, T0, mask, out_0, out_1):
+    nc = tc.nc
+    with contextlib.ExitStack() as ctx:
+        const = ctx.enter_context(tc.tile_pool(name="const", bufs=1))
+        loads = ctx.enter_context(tc.tile_pool(name="loads", bufs=1))
+        work = ctx.enter_context(tc.tile_pool(name="work", bufs=3))
+        banks = ctx.enter_context(tc.psum_pool(name="banks", bufs=6))
+        accs = ctx.enter_context(tc.psum_pool(name="accs", bufs=2))
+        ctx.enter_context(tc.manual_schedule())
+
+        ident = const.tile([P, P], F32, name="ident")
+        make_identity(nc, ident[:])
+        zero = const.tile([P, P], F32, name="zero")
+        nc.vector.memset(zero[:], 0.0)
+        ones = const.tile([P, P], BF16, name="ones")
+        nc.vector.memset(ones[:], 1.0)
+        t0row = const.tile([P, ROWS], BF16, name="t0row")
+        nc.vector.memset(t0row[:], 0.0)
+        nc.scalar.dma_start(out=t0row[0:1, :], in_=T0.rearrange("(o r) -> o r", o=1))
+        t0b = const.tile([P, M_TILES, ROWS], F32, name="t0b")
+
+        wm = {}
+        for t in range(2):
+            for parity in range(2):
+                wm[(t, parity)] = const.tile([P, CHUNKS * CHUNK], BF16, name="wm_%d_%d" % (t, parity))
+                if parity == 0:
+                    nc.vector.memset(wm[(t, parity)][:, WIN:], 0.0)
+                else:
+                    nc.vector.memset(wm[(t, parity)][:, 0 : CHUNKS * CHUNK - WIN], 0.0)
+
+        zg = const.tile([P, PASSES, 4 * BATCH], BF16, name="zg", align_bytes=64)
+        z_codes = const.tile([P, PASSES, BATCH], U32, name="z_codes", align_bytes=64)
+        z_scales = const.tile([P, PASSES, BATCH], U8, name="z_scales", align_bytes=64)
+        x1_sb = const.tile([P, M_TILES, ROWS], F32, name="x1_sb")
+        x2_sb = const.tile([P, M_TILES, ROWS], F32, name="x2_sb")
+
+        z_sb = [loads.tile([P, K], BF16, name="z_sb%d" % m) for m in range(M_TILES)]
+        mk_sb = [loads.tile([P, WIN], BF16, name="mk_sb%d" % g) for g in range(GROUPS)]
+        t_sb = [[loads.tile([P, WIN], BF16, name="t%d_sb%d" % (t, g)) for g in range(GROUPS)] for t in range(2)]
+        new_passes = []
+        have = 0
+        for g in range(GROUPS):
+            y0, chunk0, margin, first_pass, last_pass = group_geometry(g)
+            new_passes.append(list(range(have, last_pass + 1)))
+            for dst, src in ((mk_sb[g], mask), (t_sb[0][g], T1), (t_sb[1][g], T2)):
+                for s in range(STACK):
+                    r0 = s * POS * POS + J * g
+                    nc.sync.dma_start(out=dst[s:P:STACK, :], in_=src[r0 : r0 + J, IMG * y0 : IMG * y0 + WIN])
+            if last_pass + 1 > have:
+                for m in range(M_TILES):
+                    nc.sync.dma_start(
+                        out=z_sb[m][:, K_PASS * have : K_PASS * (last_pass + 1)],
+                        in_=z[P * m : P * (m + 1), K_PASS * have : K_PASS * (last_pass + 1)],
+                    )
+                have = last_pass + 1
+
+        for h in range(2):
+            bank = banks.tile([P, 4, P], F32, name="bank", tag="bank")
+            flat = bank[:].rearrange("p a b -> p (a b)")
+            nc.tensor.matmul(out=flat, lhsT=ones[:], rhs=t0row[:, 512 * h : 512 * (h + 1)], start=True, stop=True)
+            for m in range(M_TILES):
+                nc.scalar.copy(out=t0b[:, m, 512 * h : 512 * (h + 1)], in_=flat)
+
+        def z_prepare(c):
+            bank = banks.tile([P, 4, P], F32, name="bank", tag="bank")
+            for m in range(M_TILES):
+                words = z_sb[m][:].bitcast(F32)
+                for u in range(2):
+                    w0 = (2 * c + u) * P
+                    nc.tensor.transpose(bank[:, 2 * m + u, :], words[:, w0 : w0 + P], ident[:])
+            nc.scalar.copy(
+                out=zg[:, c, :].bitcast(F32).rearrange("p (m b u) -> p m b u", m=M_TILES, u=2),
+                in_=bank[:].rearrange("p (m u) b -> p m b u", u=2),
+            )
+
+        def z_quantise(c):
+            nc.vector.quantize_mx(out=z_codes[:, c, :].bitcast(FP8X4), scales=z_scales[:, c, :], in_=zg[:, c, :])
+
+        state = {}
+
+        def front(g):
+            y0, chunk0, margin, first_pass, last_pass = group_geometry(g)
+            n_pass = last_pass - first_pass + 1
+            for t in range(2):
+                nc.vector.tensor_tensor(
+                    out=wm[(t, g % 2)][:, margin : margin + WIN], in0=t_sb[t][g][:], in1=mk_sb[g][:], op=MULT
+                )
+            wg = work.tile([P, 4, 4 * 2 * P], BF16, name="wg", tag="wg", align_bytes=64)
+            for i in range(n_pass):
+                bank = banks.tile([P, 4, P], F32, name="bank", tag="bank")
+                for t in range(2):
+                    words = wm[(t, g % 2)][:].bitcast(F32)
+                    for u in range(2):
+                        ch = 2 * (first_pass + i) + u - chunk0
+                        if 0 <= ch < CHUNKS:
+                            nc.tensor.transpose(bank[:, 2 * t + u, :], words[:, P * ch : P * (ch + 1)], ident[:])
+                        else:
+                            nc.tensor.transpose(bank[:, 2 * t + u, :], zero[:], ident[:])
+                nc.scalar.copy(
+                    out=wg[:, i, :].bitcast(F32).rearrange("p (t n u) -> p t n u", t=2, u=2),
+                    in_=bank[:].rearrange("p (t u) n -> p t n u", u=2),
+                )
+            state[g] = wg
+
+        def middle(g):
+            y0, chunk0, margin, first_pass, last_pass = group_geometry(g)
+            n_pass = last_pass - first_pass + 1
+            wg = state[g]
+            w_codes = work.tile([P, 4, 2 * P], U32, name="w_codes", tag="w_codes", align_bytes=64)
+            w_scales = work.tile([P, 4, 2 * P], U8, name="w_scales", tag="w_scales", align_bytes=64)
+            cuts = [(0, 4)] if n_pass == 4 else [(0, 2), (2, 3)]
+            for a, b in cuts:
+                nc.vector.quantize_mx(
+                    out=w_codes[:, a:b, :].rearrange("p a n -> p (a n)").bitcast(FP8X4),
+                    scales=w_scales[:, a:b, :].rearrange("p a n -> p (a n)"),
+                    in_=wg[:, a:b, :].rearrange("p a n -> p (a n)"),
+                )
+            acc = accs.tile([P, M_TILES, 2 * P], F32, name="acc", tag="acc")
+            for m in range(M_TILES):
+                for i in range(n_pass):
+                    c = first_pass + i
+                    nc.tensor.matmul_mx(
+                        out=acc[:, m, :],
+                        lhsT=z_codes[:, c, P * m : P * (m + 1)].bitcast(FP8X4),
+                        lhsT_scale=z_scales[:, c, P * m : P * (m + 1)],
+                        rhs=w_codes[:, i, :].bitcast(FP8X4),
+                        rhs_scale=w_scales[:, i, :],
+                        start=(i == 0),
+                        stop=(i == n_pass - 1),
+                    )
+            state[g] = acc
+
+        def views(g):
+            acc_v = state[g][:].rearrange("p m (t j s) -> p m t s j", t=2, s=STACK)
+            x1_v = x1_sb[:].rearrange("p m (s g j) -> p m s g j", s=STACK, g=GROUPS)[:, :, :, g, :]
+            x2_v = x2_sb[:].rearrange("p m (s g j) -> p m s g j", s=STACK, g=GROUPS)[:, :, :, g, :]
+            return acc_v, x1_v, x2_v
+
+        def x1_out(g):
+            acc_v, x1_v, x2_v = views(g)
+            nc.scalar.copy(out=x1_v, in_=acc_v[:, :, 0])
+
+        def x2_product(g):
+            acc_v, x1_v, x2_v = views(g)
+            nc.vector.tensor_tensor(out=x2_v, in0=acc_v[:, :, 1], in1=x1_v, op=MULT)
+
+        def store(ga, gb):
+            x2_r = x2_sb[:].rearrange("p m (s c) -> p (m s) c", s=STACK)[:, :, J * ga : J * gb]
+            t0_r = t0b[:].rearrange("p m (s c) -> p (m s) c", s=STACK)[:, :, J * ga : J * gb]
+            nc.vector.scalar_tensor_tensor(out=x2_r, in0=x2_r, scalar=2.0, in1=t0_r, op0=MULT, op1=SUBTRACT)
+            for sb, dram in ((x1_sb, out_0), (x2_sb, out_1)):
+                for m in range(M_TILES):
+                    nc.sync.dma_start(
+                        out=dram[P * m : P * (m + 1), :].rearrange("p (s c) -> p s c", s=STACK)[:, :, J * ga : J * gb],
+                        in_=sb[:, m, :].rearrange("p (s c) -> p s c", s=STACK)[:, :, J * ga : J * gb],
+                    )
+
+        store_after = {3: (0, 4), 5: (4, 6), 7: (6, 8)}
+        for step in range(GROUPS + 2):
+            if step >= 2:
+                x1_out(step - 2)
+            if step < GROUPS:
+                front(step)
+                for c in new_passes[step]:
+                    z_prepare(c)
+            if 1 <= step <= GROUPS:
+                for c in new_passes[step - 1]:
+                    z_quantise(c)
+                middle(step - 1)
+            if step >= 2:
+                x2_product(step - 2)
+                if step - 2 in store_after:
+                    store(*store_after[step - 2])

@@ -37,6 +37,17 @@ FLOPS = 2 * 2 * BATCH * ROWS * PATCH * PATCH
 BYTES = 2 * BATCH * K + 3 * 2 * ROWS * PATCH * PATCH + 2 * ROWS + 2 * 4 * BATCH * ROWS
 
 
+LOAD_UNITS = {0: 1, 1: 1, 2: 2, 4: 2, 6: 2}
+
+
+def windows(src, s, g, n):
+    pitch = J * K + IMG * STRIDE * PY_PER_GROUP
+    base = s * POS * POS * K + g * pitch
+    flat = src.rearrange("r k -> (r k)")[base : base + n * pitch]
+    rows = flat.rearrange("(g x) -> g x", x=pitch)[:, 0 : J * K]
+    return rows.rearrange("g (j k) -> j g k", k=K)[:, :, 0:WIN]
+
+
 def group_geometry(g):
     y0 = STRIDE * PY_PER_GROUP * g
     chunk0 = y0 // CHUNK_Y
@@ -83,17 +94,30 @@ def tile_chebyshev_l3_sparsed32_stack_pa_kernel(tc, z, T1, T2, T0, mask, out_0, 
         x2_sb = const.tile([P, M_TILES, ROWS], F32, name="x2_sb")
 
         z_sb = [loads.tile([P, K], BF16, name="z_sb%d" % m) for m in range(M_TILES)]
-        mk_sb = [loads.tile([P, WIN], BF16, name="mk_sb%d" % g) for g in range(GROUPS)]
-        t_sb = [[loads.tile([P, WIN], BF16, name="t%d_sb%d" % (t, g)) for g in range(GROUPS)] for t in range(2)]
+        mk_sb = {}
+        t_sb = ({}, {})
         new_passes = []
         have = 0
         for g in range(GROUPS):
             y0, chunk0, margin, first_pass, last_pass = group_geometry(g)
             new_passes.append(list(range(have, last_pass + 1)))
-            for dst, src in ((mk_sb[g], mask), (t_sb[0][g], T1), (t_sb[1][g], T2)):
-                for s in range(STACK):
-                    r0 = s * POS * POS + J * g
-                    nc.sync.dma_start(out=dst[s:P:STACK, :], in_=src[r0 : r0 + J, IMG * y0 : IMG * y0 + WIN])
+            if g in LOAD_UNITS:
+                n = LOAD_UNITS[g]
+                for which, src in ((2, mask), (0, T1), (1, T2)):
+                    unit = loads.tile([P, n, WIN], BF16, name="ld%d_%d" % (which, g))
+                    for i in range(n):
+                        if which == 2:
+                            mk_sb[g + i] = unit[:, i, :]
+                        else:
+                            t_sb[which][g + i] = unit[:, i, :]
+                    for s in range(STACK):
+                        if n > 1 and s * POS * POS * K + (g + n) * (J * K + IMG * STRIDE * PY_PER_GROUP) <= ROWS * K:
+                            nc.sync.dma_start(out=unit[s:P:STACK, :, :], in_=windows(src, s, g, n))
+                        else:
+                            for i in range(n):
+                                r0 = s * POS * POS + J * (g + i)
+                                c0 = IMG * STRIDE * PY_PER_GROUP * (g + i)
+                                nc.sync.dma_start(out=unit[s:P:STACK, i, :], in_=src[r0 : r0 + J, c0 : c0 + WIN])
             if last_pass + 1 > have:
                 for m in range(M_TILES):
                     nc.sync.dma_start(
@@ -131,7 +155,7 @@ def tile_chebyshev_l3_sparsed32_stack_pa_kernel(tc, z, T1, T2, T0, mask, out_0, 
             n_pass = last_pass - first_pass + 1
             for t in range(2):
                 nc.vector.tensor_tensor(
-                    out=wm[(t, g % 2)][:, margin : margin + WIN], in0=t_sb[t][g][:], in1=mk_sb[g][:], op=MULT
+                    out=wm[(t, g % 2)][:, margin : margin + WIN], in0=t_sb[t][g], in1=mk_sb[g], op=MULT
                 )
             wg = work.tile([P, 4, 4 * 2 * P], BF16, name="wg", tag="wg", align_bytes=64)
             for i in range(n_pass):

@@ -37,17 +37,6 @@ FLOPS = 2 * 2 * BATCH * ROWS * PATCH * PATCH
 BYTES = 2 * BATCH * K + 3 * 2 * ROWS * PATCH * PATCH + 2 * ROWS + 2 * 4 * BATCH * ROWS
 
 
-LOAD_UNITS = {0: 1, 1: 1, 2: 2, 4: 2, 6: 2}
-
-
-def windows(src, s, g, n):
-    pitch = J * K + IMG * STRIDE * PY_PER_GROUP
-    base = s * POS * POS * K + g * pitch
-    flat = src.rearrange("r k -> (r k)")[base : base + n * pitch]
-    rows = flat.rearrange("(g x) -> g x", x=pitch)[:, 0 : J * K]
-    return rows.rearrange("g (j k) -> j g k", k=K)[:, :, 0:WIN]
-
-
 def group_geometry(g):
     y0 = STRIDE * PY_PER_GROUP * g
     chunk0 = y0 // CHUNK_Y
@@ -94,30 +83,17 @@ def tile_chebyshev_l3_sparsed32_stack_pa_kernel(tc, z, T1, T2, T0, mask, out_0, 
         x2_sb = const.tile([P, M_TILES, ROWS], F32, name="x2_sb")
 
         z_sb = [loads.tile([P, K], BF16, name="z_sb%d" % m) for m in range(M_TILES)]
-        mk_sb = {}
-        t_sb = ({}, {})
+        mk_sb = [loads.tile([P, WIN], BF16, name="mk_sb%d" % g) for g in range(GROUPS)]
+        t_sb = [[loads.tile([P, WIN], BF16, name="t%d_sb%d" % (t, g)) for g in range(GROUPS)] for t in range(2)]
         new_passes = []
         have = 0
         for g in range(GROUPS):
             y0, chunk0, margin, first_pass, last_pass = group_geometry(g)
             new_passes.append(list(range(have, last_pass + 1)))
-            if g in LOAD_UNITS:
-                n = LOAD_UNITS[g]
-                for which, src in ((2, mask), (0, T1), (1, T2)):
-                    unit = loads.tile([P, n, WIN], BF16, name="ld%d_%d" % (which, g))
-                    for i in range(n):
-                        if which == 2:
-                            mk_sb[g + i] = unit[:, i, :]
-                        else:
-                            t_sb[which][g + i] = unit[:, i, :]
-                    for s in range(STACK):
-                        if n > 1 and s * POS * POS * K + (g + n) * (J * K + IMG * STRIDE * PY_PER_GROUP) <= ROWS * K:
-                            nc.sync.dma_start(out=unit[s:P:STACK, :, :], in_=windows(src, s, g, n))
-                        else:
-                            for i in range(n):
-                                r0 = s * POS * POS + J * (g + i)
-                                c0 = IMG * STRIDE * PY_PER_GROUP * (g + i)
-                                nc.sync.dma_start(out=unit[s:P:STACK, i, :], in_=src[r0 : r0 + J, c0 : c0 + WIN])
+            for dst, src in ((mk_sb[g], mask), (t_sb[0][g], T1), (t_sb[1][g], T2)):
+                for s in range(STACK):
+                    r0 = s * POS * POS + J * g
+                    nc.sync.dma_start(out=dst[s:P:STACK, :], in_=src[r0 : r0 + J, IMG * y0 : IMG * y0 + WIN])
             if last_pass + 1 > have:
                 for m in range(M_TILES):
                     nc.sync.dma_start(
@@ -155,7 +131,7 @@ def tile_chebyshev_l3_sparsed32_stack_pa_kernel(tc, z, T1, T2, T0, mask, out_0, 
             n_pass = last_pass - first_pass + 1
             for t in range(2):
                 nc.vector.tensor_tensor(
-                    out=wm[(t, g % 2)][:, margin : margin + WIN], in0=t_sb[t][g], in1=mk_sb[g], op=MULT
+                    out=wm[(t, g % 2)][:, margin : margin + WIN], in0=t_sb[t][g][:], in1=mk_sb[g][:], op=MULT
                 )
             wg = work.tile([P, 4, 4 * 2 * P], BF16, name="wg", tag="wg", align_bytes=64)
             for i in range(n_pass):
@@ -227,14 +203,14 @@ def tile_chebyshev_l3_sparsed32_stack_pa_kernel(tc, z, T1, T2, T0, mask, out_0, 
                         in_=sb[:, m, :].rearrange("p (s c) -> p s c", s=STACK)[:, :, J * ga : J * gb],
                     )
 
-        store_after = {3: (0, 4), 5: (4, 6), 7: (6, 8)}
+        store_after = {3: (0, 4), 5: (4, 6), 6: (6, 7), 7: (7, 8)}
         for step in range(GROUPS + 2):
             if step >= 2:
                 x1_out(step - 2)
             if step < GROUPS:
-                front(step)
                 for c in new_passes[step]:
                     z_prepare(c)
+                front(step)
             if 1 <= step <= GROUPS:
                 for c in new_passes[step - 1]:
                     z_quantise(c)

@@ -64,7 +64,6 @@ def tile_chebyshev_l3_sparsed32_stack_pa_kernel(tc, z, T1, T2, T0, mask, out_0, 
         nc.vector.memset(ones[:], 1.0)
         t0row = const.tile([P, ROWS], BF16, name="t0row")
         nc.vector.memset(t0row[:], 0.0)
-        nc.scalar.dma_start(out=t0row[0:1, :], in_=T0.rearrange("(o r) -> o r", o=1))
         t0b = const.tile([P, M_TILES, ROWS], F32, name="t0b")
 
         wm = {}
@@ -101,13 +100,19 @@ def tile_chebyshev_l3_sparsed32_stack_pa_kernel(tc, z, T1, T2, T0, mask, out_0, 
                         in_=z[P * m : P * (m + 1), K_PASS * have : K_PASS * (last_pass + 1)],
                     )
                 have = last_pass + 1
+            if g == 1:
+                nc.sync.dma_start(out=t0row[0:1, :], in_=T0.rearrange("(o r) -> o r", o=1))
 
-        for h in range(2):
-            bank = banks.tile([P, 4, P], F32, name="bank", tag="bank")
-            flat = bank[:].rearrange("p a b -> p (a b)")
-            nc.tensor.matmul(out=flat, lhsT=ones[:], rhs=t0row[:, 512 * h : 512 * (h + 1)], start=True, stop=True)
-            for m in range(M_TILES):
-                nc.scalar.copy(out=t0b[:, m, 512 * h : 512 * (h + 1)], in_=flat)
+        warm = const.tile([P, 1], F32, name="warm")
+        nc.scalar.copy(out=warm[:], in_=zero[:, 0:1])
+
+        def spread_t0():
+            for h in range(2):
+                bank = banks.tile([P, 4, P], F32, name="bank", tag="bank")
+                flat = bank[:].rearrange("p a b -> p (a b)")
+                nc.tensor.matmul(out=flat, lhsT=ones[:], rhs=t0row[:, 512 * h : 512 * (h + 1)], start=True, stop=True)
+                for m in range(M_TILES):
+                    nc.scalar.copy(out=t0b[:, m, 512 * h : 512 * (h + 1)], in_=flat)
 
         def z_prepare(c):
             bank = banks.tile([P, 4, P], F32, name="bank", tag="bank")
@@ -207,6 +212,8 @@ def tile_chebyshev_l3_sparsed32_stack_pa_kernel(tc, z, T1, T2, T0, mask, out_0, 
         for step in range(GROUPS + 2):
             if step >= 2:
                 x1_out(step - 2)
+            if step == 3:
+                spread_t0()
             if step < GROUPS:
                 for c in new_passes[step]:
                     z_prepare(c)

@@ -203,7 +203,7 @@ def tile_chebyshev_l3_sparsed32_stack_pa_kernel(tc, z, T1, T2, T0, mask, out_0, 
             nc.vector.scalar_tensor_tensor(out=x2_r, in0=x2_r, scalar=2.0, in1=t0_r, op0=MULT, op1=SUBTRACT)
             for sb, dram in ((x1_sb, out_0), (x2_sb, out_1)):
                 for m in range(M_TILES):
-                    nc.sync.dma_start(
+                    (nc.sync if gb > 4 else nc.gpsimd).dma_start(
                         out=dram[P * m : P * (m + 1), :].rearrange("p (s c) -> p s c", s=STACK)[:, :, J * ga : J * gb],
                         in_=sb[:, m, :].rearrange("p (s c) -> p s c", s=STACK)[:, :, J * ga : J * gb],
                     )

@@ -81,7 +81,7 @@ def tile_chebyshev_l3_sparsed32_stack_pa_kernel(tc, z, T1, T2, T0, mask, out_0, 
         x1_sb = const.tile([P, M_TILES, ROWS], F32, name="x1_sb")
         x2_sb = const.tile([P, M_TILES, ROWS], F32, name="x2_sb")
 
-        z_sb = [loads.tile([P, K], BF16, name="z_sb%d" % m) for m in range(M_TILES)]
+        z_sb = loads.tile([P, M_TILES, K], BF16, name="z_sb")
         mk_sb = [loads.tile([P, WIN], BF16, name="mk_sb%d" % g) for g in range(GROUPS)]
         t_sb = [[loads.tile([P, WIN], BF16, name="t%d_sb%d" % (t, g)) for g in range(GROUPS)] for t in range(2)]
         new_passes = []
@@ -94,11 +94,10 @@ def tile_chebyshev_l3_sparsed32_stack_pa_kernel(tc, z, T1, T2, T0, mask, out_0, 
                     r0 = s * POS * POS + J * g
                     nc.sync.dma_start(out=dst[s:P:STACK, :], in_=src[r0 : r0 + J, IMG * y0 : IMG * y0 + WIN])
             if last_pass + 1 > have:
-                for m in range(M_TILES):
-                    nc.sync.dma_start(
-                        out=z_sb[m][:, K_PASS * have : K_PASS * (last_pass + 1)],
-                        in_=z[P * m : P * (m + 1), K_PASS * have : K_PASS * (last_pass + 1)],
-                    )
+                nc.sync.dma_start(
+                    out=z_sb[:, :, K_PASS * have : K_PASS * (last_pass + 1)],
+                    in_=z.rearrange("(m p) k -> p m k", p=P)[:, :, K_PASS * have : K_PASS * (last_pass + 1)],
+                )
                 have = last_pass + 1
             if g == 1:
                 nc.sync.dma_start(out=t0row[0:1, :], in_=T0.rearrange("(o r) -> o r", o=1))
@@ -117,7 +116,7 @@ def tile_chebyshev_l3_sparsed32_stack_pa_kernel(tc, z, T1, T2, T0, mask, out_0, 
         def z_prepare(c):
             bank = banks.tile([P, 4, P], F32, name="bank", tag="bank")
             for m in range(M_TILES):
-                words = z_sb[m][:].bitcast(F32)
+                words = z_sb[:, m, :].bitcast(F32)
                 for u in range(2):
                     w0 = (2 * c + u) * P
                     nc.tensor.transpose(bank[:, 2 * m + u, :], words[:, w0 : w0 + P], ident[:])
@@ -203,7 +202,7 @@ def tile_chebyshev_l3_sparsed32_stack_pa_kernel(tc, z, T1, T2, T0, mask, out_0, 
             nc.vector.scalar_tensor_tensor(out=x2_r, in0=x2_r, scalar=2.0, in1=t0_r, op0=MULT, op1=SUBTRACT)
             for sb, dram in ((x1_sb, out_0), (x2_sb, out_1)):
                 for m in range(M_TILES):
-                    (nc.sync if gb > 4 else nc.gpsimd).dma_start(
+                    nc.sync.dma_start(
                         out=dram[P * m : P * (m + 1), :].rearrange("p (s c) -> p s c", s=STACK)[:, :, J * ga : J * gb],
                         in_=sb[:, m, :].rearrange("p (s c) -> p s c", s=STACK)[:, :, J * ga : J * gb],
                     )

@@ -81,7 +81,7 @@ def tile_chebyshev_l3_sparsed32_stack_pa_kernel(tc, z, T1, T2, T0, mask, out_0, 
         x1_sb = const.tile([P, M_TILES, ROWS], F32, name="x1_sb")
         x2_sb = const.tile([P, M_TILES, ROWS], F32, name="x2_sb")
 
-        z_sb = loads.tile([P, M_TILES, K], BF16, name="z_sb")
+        z_sb = {}
         mk_sb = [loads.tile([P, WIN], BF16, name="mk_sb%d" % g) for g in range(GROUPS)]
         t_sb = [[loads.tile([P, WIN], BF16, name="t%d_sb%d" % (t, g)) for g in range(GROUPS)] for t in range(2)]
         new_passes = []
@@ -94,10 +94,13 @@ def tile_chebyshev_l3_sparsed32_stack_pa_kernel(tc, z, T1, T2, T0, mask, out_0, 
                     r0 = s * POS * POS + J * g
                     nc.sync.dma_start(out=dst[s:P:STACK, :], in_=src[r0 : r0 + J, IMG * y0 : IMG * y0 + WIN])
             if last_pass + 1 > have:
+                z_part = loads.tile([P, M_TILES, K_PASS * (last_pass + 1 - have)], BF16, name="z_part%d" % g)
                 nc.sync.dma_start(
-                    out=z_sb[:, :, K_PASS * have : K_PASS * (last_pass + 1)],
+                    out=z_part[:],
                     in_=z.rearrange("(m p) k -> p m k", p=P)[:, :, K_PASS * have : K_PASS * (last_pass + 1)],
                 )
+                for c in range(have, last_pass + 1):
+                    z_sb[c] = (z_part, K_PASS * (c - have))
                 have = last_pass + 1
             if g == 1:
                 nc.sync.dma_start(out=t0row[0:1, :], in_=T0.rearrange("(o r) -> o r", o=1))
@@ -115,10 +118,11 @@ def tile_chebyshev_l3_sparsed32_stack_pa_kernel(tc, z, T1, T2, T0, mask, out_0, 
 
         def z_prepare(c):
             bank = banks.tile([P, 4, P], F32, name="bank", tag="bank")
+            z_part, k0 = z_sb[c]
             for m in range(M_TILES):
-                words = z_sb[:, m, :].bitcast(F32)
+                words = z_part[:, m, :].bitcast(F32)
                 for u in range(2):
-                    w0 = (2 * c + u) * P
+                    w0 = k0 // 2 + u * P
                     nc.tensor.transpose(bank[:, 2 * m + u, :], words[:, w0 : w0 + P], ident[:])
             nc.scalar.copy(
                 out=zg[:, c, :].bitcast(F32).rearrange("p (m b u) -> p m b u", m=M_TILES, u=2),

@@ -90,9 +90,8 @@ def tile_chebyshev_l3_sparsed32_stack_pa_kernel(tc, z, T1, T2, T0, mask, out_0, 
             y0, chunk0, margin, first_pass, last_pass = group_geometry(g)
             new_passes.append(list(range(have, last_pass + 1)))
             for dst, src in ((mk_sb[g], mask), (t_sb[0][g], T1), (t_sb[1][g], T2)):
-                for s in range(STACK):
-                    r0 = s * POS * POS + J * g
-                    nc.sync.dma_start(out=dst[s:P:STACK, :], in_=src[r0 : r0 + J, IMG * y0 : IMG * y0 + WIN])
+                rows = src.rearrange("(s g j) k -> g j s k", s=STACK, g=GROUPS)
+                nc.sync.dma_start(out=dst[:], in_=rows[g, :, :, IMG * y0 : IMG * y0 + WIN])
             if last_pass + 1 > have:
                 z_part = loads.tile([P, M_TILES, K_PASS * (last_pass + 1 - have)], BF16, name="z_part%d" % g)
                 nc.sync.dma_start(

@@ -52,18 +52,19 @@ def tile_chebyshev_l3_sparsed32_stack_pa_kernel(tc, z, T1, T2, T0, mask, out_0, 
         const = ctx.enter_context(tc.tile_pool(name="const", bufs=1))
         loads = ctx.enter_context(tc.tile_pool(name="loads", bufs=1))
         work = ctx.enter_context(tc.tile_pool(name="work", bufs=3))
-        banks = ctx.enter_context(tc.psum_pool(name="banks", bufs=6))
+        banks = ctx.enter_context(tc.psum_pool(name="banks", bufs=4))
+        halves = ctx.enter_context(tc.psum_pool(name="halves", bufs=1))
         accs = ctx.enter_context(tc.psum_pool(name="accs", bufs=2))
         ctx.enter_context(tc.manual_schedule())
 
+        t0row = const.tile([P, ROWS], BF16, name="t0row")
+        nc.vector.memset(t0row[:], 0.0)
+        ones = const.tile([P, P], BF16, name="ones")
+        nc.vector.memset(ones[:], 1.0)
         ident = const.tile([P, P], F32, name="ident")
         make_identity(nc, ident[:])
         zero = const.tile([P, P], F32, name="zero")
         nc.vector.memset(zero[:], 0.0)
-        ones = const.tile([P, P], BF16, name="ones")
-        nc.vector.memset(ones[:], 1.0)
-        t0row = const.tile([P, ROWS], BF16, name="t0row")
-        nc.vector.memset(t0row[:], 0.0)
         t0b = const.tile([P, M_TILES, ROWS], F32, name="t0b")
 
         wm = {}
@@ -89,9 +90,11 @@ def tile_chebyshev_l3_sparsed32_stack_pa_kernel(tc, z, T1, T2, T0, mask, out_0, 
         for g in range(GROUPS):
             y0, chunk0, margin, first_pass, last_pass = group_geometry(g)
             new_passes.append(list(range(have, last_pass + 1)))
-            for dst, src in ((mk_sb[g], mask), (t_sb[0][g], T1), (t_sb[1][g], T2)):
+            for n, (dst, src) in enumerate(((mk_sb[g], mask), (t_sb[0][g], T1), (t_sb[1][g], T2))):
                 rows = src.rearrange("(s g j) k -> g j s k", s=STACK, g=GROUPS)
                 nc.sync.dma_start(out=dst[:], in_=rows[g, :, :, IMG * y0 : IMG * y0 + WIN])
+                if g == 0 and n == 0:
+                    nc.sync.dma_start(out=t0row[0:1, :], in_=T0.rearrange("(o r) -> o r", o=1))
             if last_pass + 1 > have:
                 z_part = loads.tile([P, M_TILES, K_PASS * (last_pass + 1 - have)], BF16, name="z_part%d" % g)
                 nc.sync.dma_start(
@@ -101,8 +104,6 @@ def tile_chebyshev_l3_sparsed32_stack_pa_kernel(tc, z, T1, T2, T0, mask, out_0, 
                 for c in range(have, last_pass + 1):
                     z_sb[c] = (z_part, K_PASS * (c - have))
                 have = last_pass + 1
-            if g == 1:
-                nc.sync.dma_start(out=t0row[0:1, :], in_=T0.rearrange("(o r) -> o r", o=1))
 
         warm = const.tile([P, 1], F32, name="warm")
         nc.scalar.copy(out=warm[:], in_=zero[:, 0:1])
@@ -114,6 +115,13 @@ def tile_chebyshev_l3_sparsed32_stack_pa_kernel(tc, z, T1, T2, T0, mask, out_0, 
                 nc.tensor.matmul(out=flat, lhsT=ones[:], rhs=t0row[:, 512 * h : 512 * (h + 1)], start=True, stop=True)
                 for m in range(M_TILES):
                     nc.scalar.copy(out=t0b[:, m, 512 * h : 512 * (h + 1)], in_=flat)
+
+        half_bank = []
+        for u_zero in range(2):
+            bank = halves.tile([P, 4, P], F32, name="half_bank%d" % u_zero)
+            for t in range(2):
+                nc.tensor.transpose(bank[:, 2 * t + u_zero, :], zero[:], ident[:])
+            half_bank.append(bank)
 
         def z_prepare(c):
             bank = banks.tile([P, 4, P], F32, name="bank", tag="bank")
@@ -142,22 +150,23 @@ def tile_chebyshev_l3_sparsed32_stack_pa_kernel(tc, z, T1, T2, T0, mask, out_0, 
                 )
             wg = work.tile([P, 4, 4 * 2 * P], BF16, name="wg", tag="wg", align_bytes=64)
             for i in range(n_pass):
-                bank = banks.tile([P, 4, P], F32, name="bank", tag="bank")
+                inside = [u for u in range(2) if 0 <= 2 * (first_pass + i) + u - chunk0 < CHUNKS]
+                if len(inside) == 2:
+                    bank = banks.tile([P, 4, P], F32, name="bank", tag="bank")
+                else:
+                    bank = half_bank[1 - inside[0]]
                 for t in range(2):
                     words = wm[(t, g % 2)][:].bitcast(F32)
-                    for u in range(2):
+                    for u in inside:
                         ch = 2 * (first_pass + i) + u - chunk0
-                        if 0 <= ch < CHUNKS:
-                            nc.tensor.transpose(bank[:, 2 * t + u, :], words[:, P * ch : P * (ch + 1)], ident[:])
-                        else:
-                            nc.tensor.transpose(bank[:, 2 * t + u, :], zero[:], ident[:])
+                        nc.tensor.transpose(bank[:, 2 * t + u, :], words[:, P * ch : P * (ch + 1)], ident[:])
                 nc.scalar.copy(
                     out=wg[:, i, :].bitcast(F32).rearrange("p (t n u) -> p t n u", t=2, u=2),
                     in_=bank[:].rearrange("p (t u) n -> p t n u", u=2),
                 )
             state[g] = wg
 
-        def middle(g):
+        def w_quantise(g):
             y0, chunk0, margin, first_pass, last_pass = group_geometry(g)
             n_pass = last_pass - first_pass + 1
             wg = state[g]
@@ -170,6 +179,12 @@ def tile_chebyshev_l3_sparsed32_stack_pa_kernel(tc, z, T1, T2, T0, mask, out_0, 
                     scales=w_scales[:, a:b, :].rearrange("p a n -> p (a n)"),
                     in_=wg[:, a:b, :].rearrange("p a n -> p (a n)"),
                 )
+            state[g] = (w_codes, w_scales)
+
+        def multiply(g):
+            y0, chunk0, margin, first_pass, last_pass = group_geometry(g)
+            n_pass = last_pass - first_pass + 1
+            w_codes, w_scales = state[g]
             acc = accs.tile([P, M_TILES, 2 * P], F32, name="acc", tag="acc")
             for m in range(M_TILES):
                 for i in range(n_pass):
@@ -211,19 +226,26 @@ def tile_chebyshev_l3_sparsed32_stack_pa_kernel(tc, z, T1, T2, T0, mask, out_0, 
                     )
 
         store_after = {3: (0, 4), 5: (4, 6), 6: (6, 7), 7: (7, 8)}
+        spread_t0()
         for step in range(GROUPS + 2):
             if step >= 2:
                 x1_out(step - 2)
-            if step == 3:
-                spread_t0()
-            if step < GROUPS:
+            if step == 0:
+                front(0)
+                for c in new_passes[0]:
+                    z_prepare(c)
+            elif step < GROUPS:
+                if step == 1:
+                    w_quantise(0)
                 for c in new_passes[step]:
                     z_prepare(c)
                 front(step)
             if 1 <= step <= GROUPS:
                 for c in new_passes[step - 1]:
                     z_quantise(c)
-                middle(step - 1)
+                if step > 1:
+                    w_quantise(step - 1)
+                multiply(step - 1)
             if step >= 2:
                 x2_product(step - 2)
                 if step - 2 in store_after:

@@ -214,22 +214,26 @@ def tile_chebyshev_l3_sparsed32_stack_pa_kernel(tc, z, T1, T2, T0, mask, out_0, 
             acc_v, x1_v, x2_v = views(g)
             nc.vector.tensor_tensor(out=x2_v, in0=acc_v[:, :, 1], in1=x1_v, op=MULT)
 
-        def store(ga, gb):
+        def store(sb, dram, ga, gb):
+            for m in range(M_TILES):
+                nc.sync.dma_start(
+                    out=dram[P * m : P * (m + 1), :].rearrange("p (s c) -> p s c", s=STACK)[:, :, J * ga : J * gb],
+                    in_=sb[:, m, :].rearrange("p (s c) -> p s c", s=STACK)[:, :, J * ga : J * gb],
+                )
+
+        def x2_finish(ga, gb):
             x2_r = x2_sb[:].rearrange("p m (s c) -> p (m s) c", s=STACK)[:, :, J * ga : J * gb]
             t0_r = t0b[:].rearrange("p m (s c) -> p (m s) c", s=STACK)[:, :, J * ga : J * gb]
             nc.vector.scalar_tensor_tensor(out=x2_r, in0=x2_r, scalar=2.0, in1=t0_r, op0=MULT, op1=SUBTRACT)
-            for sb, dram in ((x1_sb, out_0), (x2_sb, out_1)):
-                for m in range(M_TILES):
-                    nc.sync.dma_start(
-                        out=dram[P * m : P * (m + 1), :].rearrange("p (s c) -> p s c", s=STACK)[:, :, J * ga : J * gb],
-                        in_=sb[:, m, :].rearrange("p (s c) -> p s c", s=STACK)[:, :, J * ga : J * gb],
-                    )
+            store(x2_sb, out_1, ga, gb)
 
         store_after = {3: (0, 4), 5: (4, 6), 6: (6, 7), 7: (7, 8)}
         spread_t0()
         for step in range(GROUPS + 2):
             if step >= 2:
                 x1_out(step - 2)
+                if step - 2 in store_after:
+                    store(x1_sb, out_0, *store_after[step - 2])
             if step == 0:
                 front(0)
                 for c in new_passes[0]:
@@ -249,4 +253,4 @@ def tile_chebyshev_l3_sparsed32_stack_pa_kernel(tc, z, T1, T2, T0, mask, out_0, 
             if step >= 2:
                 x2_product(step - 2)
                 if step - 2 in store_after:
-                    store(*store_after[step - 2])
+                    x2_finish(*store_after[step - 2])

@@ -65,7 +65,7 @@ def tile_chebyshev_l3_sparsed32_stack_pa_kernel(tc, z, T1, T2, T0, mask, out_0, 
         make_identity(nc, ident[:])
         zero = const.tile([P, P], F32, name="zero")
         nc.vector.memset(zero[:], 0.0)
-        t0b = const.tile([P, M_TILES, ROWS], F32, name="t0b")
+        t0b = const.tile([P, ROWS], BF16, name="t0b")
 
         wm = {}
         for t in range(2):
@@ -90,10 +90,10 @@ def tile_chebyshev_l3_sparsed32_stack_pa_kernel(tc, z, T1, T2, T0, mask, out_0, 
         for g in range(GROUPS):
             y0, chunk0, margin, first_pass, last_pass = group_geometry(g)
             new_passes.append(list(range(have, last_pass + 1)))
-            for n, (dst, src) in enumerate(((mk_sb[g], mask), (t_sb[0][g], T1), (t_sb[1][g], T2))):
+            for dst, src in ((mk_sb[g], mask), (t_sb[0][g], T1), (t_sb[1][g], T2)):
                 rows = src.rearrange("(s g j) k -> g j s k", s=STACK, g=GROUPS)
                 nc.sync.dma_start(out=dst[:], in_=rows[g, :, :, IMG * y0 : IMG * y0 + WIN])
-                if g == 0 and n == 0:
+                if g == 0 and src is mask:
                     nc.sync.dma_start(out=t0row[0:1, :], in_=T0.rearrange("(o r) -> o r", o=1))
             if last_pass + 1 > have:
                 z_part = loads.tile([P, M_TILES, K_PASS * (last_pass + 1 - have)], BF16, name="z_part%d" % g)
@@ -109,12 +109,11 @@ def tile_chebyshev_l3_sparsed32_stack_pa_kernel(tc, z, T1, T2, T0, mask, out_0, 
         nc.scalar.copy(out=warm[:], in_=zero[:, 0:1])
 
         def spread_t0():
+            bank = banks.tile([P, ROWS], BF16, name="t0_bank", tag="bank")
             for h in range(2):
-                bank = banks.tile([P, 4, P], F32, name="bank", tag="bank")
-                flat = bank[:].rearrange("p a b -> p (a b)")
-                nc.tensor.matmul(out=flat, lhsT=ones[:], rhs=t0row[:, 512 * h : 512 * (h + 1)], start=True, stop=True)
-                for m in range(M_TILES):
-                    nc.scalar.copy(out=t0b[:, m, 512 * h : 512 * (h + 1)], in_=flat)
+                cols = slice(512 * h, 512 * (h + 1))
+                nc.tensor.matmul(out=bank[:, cols], lhsT=ones[:], rhs=t0row[:, cols], start=True, stop=True)
+            nc.scalar.copy(out=t0b[:], in_=bank[:])
 
         half_bank = []
         for u_zero in range(2):
@@ -141,13 +140,16 @@ def tile_chebyshev_l3_sparsed32_stack_pa_kernel(tc, z, T1, T2, T0, mask, out_0, 
 
         state = {}
 
-        def front(g):
-            y0, chunk0, margin, first_pass, last_pass = group_geometry(g)
-            n_pass = last_pass - first_pass + 1
+        def products(g):
+            margin = group_geometry(g)[2]
             for t in range(2):
                 nc.vector.tensor_tensor(
                     out=wm[(t, g % 2)][:, margin : margin + WIN], in0=t_sb[t][g][:], in1=mk_sb[g][:], op=MULT
                 )
+
+        def spread_weights(g):
+            y0, chunk0, margin, first_pass, last_pass = group_geometry(g)
+            n_pass = last_pass - first_pass + 1
             wg = work.tile([P, 4, 4 * 2 * P], BF16, name="wg", tag="wg", align_bytes=64)
             for i in range(n_pass):
                 inside = [u for u in range(2) if 0 <= 2 * (first_pass + i) + u - chunk0 < CHUNKS]
@@ -206,36 +208,41 @@ def tile_chebyshev_l3_sparsed32_stack_pa_kernel(tc, z, T1, T2, T0, mask, out_0, 
             x2_v = x2_sb[:].rearrange("p m (s g j) -> p m s g j", s=STACK, g=GROUPS)[:, :, :, g, :]
             return acc_v, x1_v, x2_v
 
-        def x1_out(g):
+        def x1_out(g, ms):
             acc_v, x1_v, x2_v = views(g)
-            nc.scalar.copy(out=x1_v, in_=acc_v[:, :, 0])
+            nc.scalar.copy(out=x1_v[:, ms], in_=acc_v[:, ms, 0])
 
-        def x2_product(g):
+        def x2_product(g, ms):
             acc_v, x1_v, x2_v = views(g)
-            nc.vector.tensor_tensor(out=x2_v, in0=acc_v[:, :, 1], in1=x1_v, op=MULT)
+            nc.vector.tensor_tensor(out=x2_v[:, ms], in0=acc_v[:, ms, 1], in1=x1_v[:, ms], op=MULT)
 
-        def store(sb, dram, ga, gb):
-            for m in range(M_TILES):
-                nc.sync.dma_start(
-                    out=dram[P * m : P * (m + 1), :].rearrange("p (s c) -> p s c", s=STACK)[:, :, J * ga : J * gb],
-                    in_=sb[:, m, :].rearrange("p (s c) -> p s c", s=STACK)[:, :, J * ga : J * gb],
-                )
+        def store(sb, dram, ga, gb, m):
+            nc.sync.dma_start(
+                out=dram[P * m : P * (m + 1), :].rearrange("p (s c) -> p s c", s=STACK)[:, :, J * ga : J * gb],
+                in_=sb[:, m, :].rearrange("p (s c) -> p s c", s=STACK)[:, :, J * ga : J * gb],
+            )
 
         def x2_finish(ga, gb):
-            x2_r = x2_sb[:].rearrange("p m (s c) -> p (m s) c", s=STACK)[:, :, J * ga : J * gb]
-            t0_r = t0b[:].rearrange("p m (s c) -> p (m s) c", s=STACK)[:, :, J * ga : J * gb]
-            nc.vector.scalar_tensor_tensor(out=x2_r, in0=x2_r, scalar=2.0, in1=t0_r, op0=MULT, op1=SUBTRACT)
-            store(x2_sb, out_1, ga, gb)
+            t0_r = t0b[:].rearrange("p (s c) -> p s c", s=STACK)[:, :, J * ga : J * gb]
+            for m in range(M_TILES):
+                x2_r = x2_sb[:, m, :].rearrange("p (s c) -> p s c", s=STACK)[:, :, J * ga : J * gb]
+                nc.vector.scalar_tensor_tensor(out=x2_r, in0=x2_r, scalar=2.0, in1=t0_r, op0=MULT, op1=SUBTRACT)
+                store(x2_sb, out_1, ga, gb, m)
 
-        store_after = {3: (0, 4), 5: (4, 6), 6: (6, 7), 7: (7, 8)}
+        store_after = {3: (0, 4), 5: (4, 6), 7: (6, 8)}
         spread_t0()
         for step in range(GROUPS + 2):
-            if step >= 2:
-                x1_out(step - 2)
-                if step - 2 in store_after:
-                    store(x1_sb, out_0, *store_after[step - 2])
+            done = step - 2
+            if done >= 0:
+                pieces = [slice(0, M_TILES)] if done < GROUPS - 1 else [slice(m, m + 1) for m in range(M_TILES)]
+                for ms in pieces:
+                    x1_out(done, ms)
+                if done in store_after:
+                    for m in range(M_TILES):
+                        store(x1_sb, out_0, *store_after[done], m)
             if step == 0:
-                front(0)
+                products(0)
+                spread_weights(0)
                 for c in new_passes[0]:
                     z_prepare(c)
             elif step < GROUPS:
@@ -243,14 +250,22 @@ def tile_chebyshev_l3_sparsed32_stack_pa_kernel(tc, z, T1, T2, T0, mask, out_0, 
                     w_quantise(0)
                 for c in new_passes[step]:
                     z_prepare(c)
-                front(step)
+                products(step)
+                spread_weights(step)
+            if step < GROUPS and done - 1 in store_after:
+                x2_finish(*store_after[done - 1])
             if 1 <= step <= GROUPS:
-                for c in new_passes[step - 1]:
-                    z_quantise(c)
                 if step > 1:
                     w_quantise(step - 1)
+                for c in new_passes[step - 1]:
+                    z_quantise(c)
                 multiply(step - 1)
-            if step >= 2:
-                x2_product(step - 2)
-                if step - 2 in store_after:
-                    x2_finish(*store_after[step - 2])
+            if step >= GROUPS and done - 1 in store_after:
+                x2_finish(*store_after[done - 1])
+            if done >= 0:
+                if done < GROUPS - 1:
+                    x2_product(done, slice(0, M_TILES))
+                else:
+                    for m in range(M_TILES):
+                        x2_product(done, slice(m, m + 1))
+                    x2_finish(*store_after[done])

@@ -46,6 +46,19 @@ def group_geometry(g):
     return y0, chunk0, margin, first_pass, last_pass
 
 
+def needed(g, c, b):
+    y_first = STRIDE * (PY_PER_GROUP * g + b)
+    c_y = K_PASS // IMG
+    return y_first < c_y * (c + 1) and c_y * c < y_first + PATCH
+
+
+def pass_order(g):
+    first_pass, last_pass = group_geometry(g)[3:]
+    passes = list(range(first_pass, last_pass + 1))
+    both = [c for c in passes if needed(g, c, 0) and needed(g, c, 1)]
+    return both, [c for c in passes if c not in both]
+
+
 def tile_chebyshev_l3_sparsed32_stack_pa_kernel(tc, z, T1, T2, T0, mask, out_0, out_1):
     nc = tc.nc
     with contextlib.ExitStack() as ctx:
@@ -115,24 +128,30 @@ def tile_chebyshev_l3_sparsed32_stack_pa_kernel(tc, z, T1, T2, T0, mask, out_0, 
                 nc.tensor.matmul(out=bank[:, cols], lhsT=ones[:], rhs=t0row[:, cols], start=True, stop=True)
             nc.scalar.copy(out=t0b[:], in_=bank[:])
 
+        def quarter(bank, split, t, u):
+            if split:
+                return bank[:].rearrange("p (b t u r) -> p t u b r", b=2, t=2, u=2)[:, t, u]
+            return bank[:].rearrange("p (t u n) -> p t u n", t=2, u=2)[:, t, u]
+
         half_bank = []
         for u_zero in range(2):
-            bank = halves.tile([P, 4, P], F32, name="half_bank%d" % u_zero)
+            bank = halves.tile([P, 4 * P], F32, name="half_bank%d" % u_zero)
             for t in range(2):
-                nc.tensor.transpose(bank[:, 2 * t + u_zero, :], zero[:], ident[:])
+                nc.tensor.transpose(quarter(bank, True, t, u_zero), zero[:], ident[:])
             half_bank.append(bank)
 
         def z_prepare(c):
-            bank = banks.tile([P, 4, P], F32, name="bank", tag="bank")
+            bank = banks.tile([P, 4 * P], F32, name="bank", tag="bank")
             z_part, k0 = z_sb[c]
             for m in range(M_TILES):
                 words = z_part[:, m, :].bitcast(F32)
                 for u in range(2):
                     w0 = k0 // 2 + u * P
-                    nc.tensor.transpose(bank[:, 2 * m + u, :], words[:, w0 : w0 + P], ident[:])
+                    q = 2 * m + u
+                    nc.tensor.transpose(bank[:, P * q : P * (q + 1)], words[:, w0 : w0 + P], ident[:])
             nc.scalar.copy(
                 out=zg[:, c, :].bitcast(F32).rearrange("p (m b u) -> p m b u", m=M_TILES, u=2),
-                in_=bank[:].rearrange("p (m u) b -> p m b u", u=2),
+                in_=bank[:].rearrange("p (m u b) -> p m b u", m=M_TILES, u=2),
             )
 
         def z_quantise(c):
@@ -149,72 +168,87 @@ def tile_chebyshev_l3_sparsed32_stack_pa_kernel(tc, z, T1, T2, T0, mask, out_0, 
 
         def spread_weights(g):
             y0, chunk0, margin, first_pass, last_pass = group_geometry(g)
-            n_pass = last_pass - first_pass + 1
-            wg = work.tile([P, 4, 4 * 2 * P], BF16, name="wg", tag="wg", align_bytes=64)
-            for i in range(n_pass):
-                inside = [u for u in range(2) if 0 <= 2 * (first_pass + i) + u - chunk0 < CHUNKS]
+            both, single = pass_order(g)
+            split = len(single) > 0
+            wg = work.tile([P, 4 * 4 * 2 * P], BF16, name="wg", tag="wg", align_bytes=64)
+            for c in range(first_pass, last_pass + 1):
+                inside = [u for u in range(2) if 0 <= 2 * c + u - chunk0 < CHUNKS]
                 if len(inside) == 2:
-                    bank = banks.tile([P, 4, P], F32, name="bank", tag="bank")
+                    bank = banks.tile([P, 4 * P], F32, name="bank", tag="bank")
                 else:
                     bank = half_bank[1 - inside[0]]
                 for t in range(2):
                     words = wm[(t, g % 2)][:].bitcast(F32)
                     for u in inside:
-                        ch = 2 * (first_pass + i) + u - chunk0
-                        nc.tensor.transpose(bank[:, 2 * t + u, :], words[:, P * ch : P * (ch + 1)], ident[:])
+                        ch = 2 * c + u - chunk0
+                        nc.tensor.transpose(quarter(bank, split, t, u), words[:, P * ch : P * (ch + 1)], ident[:])
+                if c in both:
+                    src, at = bank[:], 4 * P * both.index(c)
+                else:
+                    b = 0 if needed(g, c, 0) else 1
+                    src, at = bank[:, 2 * P * b : 2 * P * (b + 1)], 4 * P * len(both)
+                n = src.shape[1]
+                r = P // 2 if split else P
                 nc.scalar.copy(
-                    out=wg[:, i, :].bitcast(F32).rearrange("p (t n u) -> p t n u", t=2, u=2),
-                    in_=bank[:].rearrange("p (t u) n -> p t n u", u=2),
+                    out=wg[:].bitcast(F32)[:, at : at + n].rearrange("p (q r u) -> p q r u", r=r, u=2),
+                    in_=src.rearrange("p (q u r) -> p q r u", r=r, u=2),
                 )
             state[g] = wg
 
         def w_quantise(g):
-            y0, chunk0, margin, first_pass, last_pass = group_geometry(g)
-            n_pass = last_pass - first_pass + 1
+            both, single = pass_order(g)
             wg = state[g]
-            w_codes = work.tile([P, 4, 2 * P], U32, name="w_codes", tag="w_codes", align_bytes=64)
-            w_scales = work.tile([P, 4, 2 * P], U8, name="w_scales", tag="w_scales", align_bytes=64)
-            cuts = [(0, 4)] if n_pass == 4 else [(0, 2), (2, 3)]
-            for a, b in cuts:
+            w_codes = work.tile([P, 4 * 2 * P], U32, name="w_codes", tag="w_codes", align_bytes=64)
+            w_scales = work.tile([P, 4 * 2 * P], U8, name="w_scales", tag="w_scales", align_bytes=64)
+            a = 0
+            for n in [4 * P, 2 * P] + [P] * len(single):
                 nc.vector.quantize_mx(
-                    out=w_codes[:, a:b, :].rearrange("p a n -> p (a n)").bitcast(FP8X4),
-                    scales=w_scales[:, a:b, :].rearrange("p a n -> p (a n)"),
-                    in_=wg[:, a:b, :].rearrange("p a n -> p (a n)"),
+                    out=w_codes[:, a : a + n].bitcast(FP8X4), scales=w_scales[:, a : a + n], in_=wg[:, 4 * a : 4 * (a + n)]
                 )
+                a += n
             state[g] = (w_codes, w_scales)
 
         def multiply(g):
-            y0, chunk0, margin, first_pass, last_pass = group_geometry(g)
-            n_pass = last_pass - first_pass + 1
+            both, single = pass_order(g)
             w_codes, w_scales = state[g]
             acc = accs.tile([P, M_TILES, 2 * P], F32, name="acc", tag="acc")
             for m in range(M_TILES):
-                for i in range(n_pass):
-                    c = first_pass + i
-                    nc.tensor.matmul_mx(
-                        out=acc[:, m, :],
-                        lhsT=z_codes[:, c, P * m : P * (m + 1)].bitcast(FP8X4),
-                        lhsT_scale=z_scales[:, c, P * m : P * (m + 1)],
-                        rhs=w_codes[:, i, :].bitcast(FP8X4),
-                        rhs_scale=w_scales[:, i, :],
-                        start=(i == 0),
-                        stop=(i == n_pass - 1),
-                    )
+                groups = [(0, 2 * P, [(c, 2 * P * i) for i, c in enumerate(both)])]
+                if single:
+                    groups = []
+                    for b in range(2):
+                        terms = [(c, 2 * P * i + P * b) for i, c in enumerate(both)]
+                        terms += [(c, 2 * P * len(both)) for c in single if needed(g, c, b)]
+                        groups.append((P * b, P, terms))
+                for n0, n, terms in groups:
+                    for i, (c, a) in enumerate(terms):
+                        nc.tensor.matmul_mx(
+                            out=acc[:, m, n0 : n0 + n],
+                            lhsT=z_codes[:, c, P * m : P * (m + 1)].bitcast(FP8X4),
+                            lhsT_scale=z_scales[:, c, P * m : P * (m + 1)],
+                            rhs=w_codes[:, a : a + n].bitcast(FP8X4),
+                            rhs_scale=w_scales[:, a : a + n],
+                            start=(i == 0),
+                            stop=(i == len(terms) - 1),
+                        )
             state[g] = acc
 
         def views(g):
-            acc_v = state[g][:].rearrange("p m (t j s) -> p m t s j", t=2, s=STACK)
             x1_v = x1_sb[:].rearrange("p m (s g j) -> p m s g j", s=STACK, g=GROUPS)[:, :, :, g, :]
             x2_v = x2_sb[:].rearrange("p m (s g j) -> p m s g j", s=STACK, g=GROUPS)[:, :, :, g, :]
-            return acc_v, x1_v, x2_v
+            if not pass_order(g)[1]:
+                acc_v = state[g][:].rearrange("p m (t j s) -> p m t s j", t=2, s=STACK)
+                return [(acc_v, x1_v, x2_v)]
+            acc_v = state[g][:].rearrange("p m (b t x s) -> p b m t s x", b=2, t=2, s=STACK)
+            return [(acc_v[:, b], x1_v[:, :, :, POS * b : POS * (b + 1)], x2_v[:, :, :, POS * b : POS * (b + 1)]) for b in range(2)]
 
         def x1_out(g, ms):
-            acc_v, x1_v, x2_v = views(g)
-            nc.scalar.copy(out=x1_v[:, ms], in_=acc_v[:, ms, 0])
+            for acc_v, x1_v, x2_v in views(g):
+                nc.scalar.copy(out=x1_v[:, ms], in_=acc_v[:, ms, 0])
 
         def x2_product(g, ms):
-            acc_v, x1_v, x2_v = views(g)
-            nc.vector.tensor_tensor(out=x2_v[:, ms], in0=acc_v[:, ms, 1], in1=x1_v[:, ms], op=MULT)
+            for acc_v, x1_v, x2_v in views(g):
+                nc.vector.tensor_tensor(out=x2_v[:, ms], in0=acc_v[:, ms, 1], in1=x1_v[:, ms], op=MULT)
 
         def store(sb, dram, ga, gb, m):
             nc.sync.dma_start(

@@ -189,7 +189,8 @@ def tile_chebyshev_l3_sparsed32_stack_pa_kernel(tc, z, T1, T2, T0, mask, out_0, 
                     src, at = bank[:, 2 * P * b : 2 * P * (b + 1)], 4 * P * len(both)
                 n = src.shape[1]
                 r = P // 2 if split else P
-                nc.scalar.copy(
+                copy = nc.vector.tensor_copy if g == 0 and c == 1 else nc.scalar.copy
+                copy(
                     out=wg[:].bitcast(F32)[:, at : at + n].rearrange("p (q r u) -> p q r u", r=r, u=2),
                     in_=src.rearrange("p (q u r) -> p q r u", r=r, u=2),
                 )

@@ -32,6 +32,7 @@ CHUNK_Y = CHUNK // IMG
 CHUNKS = 6
 K_PASS = 512
 PASSES = K // K_PASS
+OFFLOADED = 4
 
 FLOPS = 2 * 2 * BATCH * ROWS * PATCH * PATCH
 BYTES = 2 * BATCH * K + 3 * 2 * ROWS * PATCH * PATCH + 2 * ROWS + 2 * 4 * BATCH * ROWS
@@ -79,6 +80,8 @@ def tile_chebyshev_l3_sparsed32_stack_pa_kernel(tc, z, T1, T2, T0, mask, out_0, 
         zero = const.tile([P, P], F32, name="zero")
         nc.vector.memset(zero[:], 0.0)
         t0b = const.tile([P, ROWS], BF16, name="t0b")
+        minus_half = const.tile([P, P], BF16, name="minus_half")
+        nc.vector.memset(minus_half[:], -0.5)
 
         wm = {}
         for t in range(2):
@@ -251,6 +254,39 @@ def tile_chebyshev_l3_sparsed32_stack_pa_kernel(tc, z, T1, T2, T0, mask, out_0, 
             for acc_v, x1_v, x2_v in views(g):
                 nc.vector.tensor_tensor(out=x2_v[:, ms], in0=acc_v[:, ms, 1], in1=x1_v[:, ms], op=MULT)
 
+        half_x2 = {}
+
+        def half_x2_product(g):
+            prod = work.tile([P, M_TILES, P], F32, name="prod", tag="prod")
+            if pass_order(g)[1]:
+                x1_v = x1_sb[:].rearrange("p m (s g b x) -> p b m g x s", s=STACK, g=GROUPS, b=2)
+                acc_v = state[g][:].rearrange("p m (b t x s) -> p b m t x s", b=2, t=2, s=STACK)
+                out_v = prod[:].rearrange("p m (b x s) -> p b m x s", b=2, s=STACK)
+                pieces = [(out_v[:, b], acc_v[:, b, :, 1], x1_v[:, b, :, g]) for b in range(2)]
+            else:
+                x1_v = x1_sb[:].rearrange("p m (s g j) -> p m g j s", s=STACK, g=GROUPS)
+                acc_v = state[g][:].rearrange("p m (t j s) -> p m t j s", t=2, s=STACK)
+                pieces = [(prod[:].rearrange("p m (j s) -> p m j s", s=STACK), acc_v[:, :, 1], x1_v[:, :, g])]
+            for out, in0, in1 in pieces:
+                nc.vector.tensor_tensor(out=out, in0=in0, in1=in1, op=MULT)
+            half_x2[g] = prod
+
+        def half_x2_sum(g):
+            bank = banks.tile([P, 4 * P], F32, name="x2_bank", tag="bank")
+            t0_g = t0row[:].rearrange("p (s g j) -> p g j s", s=STACK, g=GROUPS)[:, g]
+            for m in range(M_TILES):
+                cols = slice(P * m, P * (m + 1))
+                nc.tensor.matmul(out=bank[:, cols], lhsT=minus_half[:], rhs=t0_g, start=True, stop=False)
+                nc.tensor.matmul(out=bank[:, cols], lhsT=ident[:], rhs=half_x2[g][:, m, :], start=False, stop=True)
+            half_x2[g] = bank
+
+        def x2_out(g):
+            nc.scalar.mul(
+                out=x2_sb[:].rearrange("p m (s g j) -> p m s g j", s=STACK, g=GROUPS)[:, :, :, g, :],
+                in_=half_x2[g][:, 0 : M_TILES * P].rearrange("p (m j s) -> p m s j", m=M_TILES, s=STACK),
+                mul=2.0,
+            )
+
         def store(sb, dram, ga, gb, m):
             nc.sync.dma_start(
                 out=dram[P * m : P * (m + 1), :].rearrange("p (s c) -> p s c", s=STACK)[:, :, J * ga : J * gb],
@@ -285,9 +321,15 @@ def tile_chebyshev_l3_sparsed32_stack_pa_kernel(tc, z, T1, T2, T0, mask, out_0, 
                     w_quantise(0)
                 for c in new_passes[step]:
                     z_prepare(c)
+                if 0 <= done - 1 < OFFLOADED:
+                    half_x2_sum(done - 1)
+                    x2_out(done - 1)
+                    if done == OFFLOADED:
+                        for m in range(M_TILES):
+                            store(x2_sb, out_1, 0, OFFLOADED, m)
                 products(step)
                 spread_weights(step)
-            if step < GROUPS and done - 1 in store_after:
+            if step < GROUPS and done > OFFLOADED and done - 1 in store_after:
                 x2_finish(*store_after[done - 1])
             if 1 <= step <= GROUPS:
                 if step > 1:
@@ -298,7 +340,9 @@ def tile_chebyshev_l3_sparsed32_stack_pa_kernel(tc, z, T1, T2, T0, mask, out_0, 
             if step >= GROUPS and done - 1 in store_after:
                 x2_finish(*store_after[done - 1])
             if done >= 0:
-                if done < GROUPS - 1:
+                if done < OFFLOADED:
+                    half_x2_product(done)
+                elif done < GROUPS - 1:
                     x2_product(done, slice(0, M_TILES))
                 else:
                     for m in range(M_TILES):

@@ -274,10 +274,12 @@ def tile_chebyshev_l3_sparsed32_stack_pa_kernel(tc, z, T1, T2, T0, mask, out_0, 
         def half_x2_sum(g):
             bank = banks.tile([P, 4 * P], F32, name="x2_bank", tag="bank")
             t0_g = t0row[:].rearrange("p (s g j) -> p g j s", s=STACK, g=GROUPS)[:, g]
-            for m in range(M_TILES):
-                cols = slice(P * m, P * (m + 1))
-                nc.tensor.matmul(out=bank[:, cols], lhsT=minus_half[:], rhs=t0_g, start=True, stop=False)
-                nc.tensor.matmul(out=bank[:, cols], lhsT=ident[:], rhs=half_x2[g][:, m, :], start=False, stop=True)
+            both_m = bank[:, 0 : M_TILES * P]
+            t0_m = t0_g.unsqueeze(1).to_broadcast([P, M_TILES, J, STACK])
+            nc.tensor.matmul(out=both_m, lhsT=minus_half[:], rhs=t0_m, start=True, stop=False)
+            nc.tensor.matmul(
+                out=both_m, lhsT=ident[:], rhs=half_x2[g][:].rearrange("p m n -> p (m n)"), start=False, stop=True
+            )
             half_x2[g] = bank
 
         def x2_out(g):

import contextlib

import concourse.mybir as mybir
from concourse.masks import make_identity

F32 = mybir.dt.float32
BF16 = mybir.dt.bfloat16
U32 = mybir.dt.uint32
U8 = mybir.dt.uint8
FP8X4 = mybir.dt.float8_e4m3fn_x4
MULT = mybir.AluOpType.mult
SUBTRACT = mybir.AluOpType.subtract

P = 128
IMG = 64
PATCH = 19
STRIDE = 3
POS = 16
STACK = 4
BATCH = 256
K = IMG * IMG
ROWS = STACK * POS * POS
M_TILES = BATCH // P

PY_PER_GROUP = 2
GROUPS = POS // PY_PER_GROUP
J = PY_PER_GROUP * POS
WIN_Y = STRIDE * (PY_PER_GROUP - 1) + PATCH
WIN = WIN_Y * IMG
CHUNK = 256
CHUNK_Y = CHUNK // IMG
CHUNKS = 6
K_PASS = 512
PASSES = K // K_PASS
OFFLOADED = 4

FLOPS = 2 * 2 * BATCH * ROWS * PATCH * PATCH
BYTES = 2 * BATCH * K + 3 * 2 * ROWS * PATCH * PATCH + 2 * ROWS + 2 * 4 * BATCH * ROWS


def group_geometry(g):
    y0 = STRIDE * PY_PER_GROUP * g
    chunk0 = y0 // CHUNK_Y
    margin = (y0 % CHUNK_Y) * IMG
    first_pass = chunk0 // 2
    last_pass = (chunk0 + CHUNKS - 1) // 2
    return y0, chunk0, margin, first_pass, last_pass


def needed(g, c, b):
    y_first = STRIDE * (PY_PER_GROUP * g + b)
    c_y = K_PASS // IMG
    return y_first < c_y * (c + 1) and c_y * c < y_first + PATCH


def pass_order(g):
    first_pass, last_pass = group_geometry(g)[3:]
    passes = list(range(first_pass, last_pass + 1))
    both = [c for c in passes if needed(g, c, 0) and needed(g, c, 1)]
    return both, [c for c in passes if c not in both]


def tile_chebyshev_l3_sparsed32_stack_pa_kernel(tc, z, T1, T2, T0, mask, out_0, out_1):
    nc = tc.nc
    with contextlib.ExitStack() as ctx:
        const = ctx.enter_context(tc.tile_pool(name="const", bufs=1))
        loads = ctx.enter_context(tc.tile_pool(name="loads", bufs=1))
        work = ctx.enter_context(tc.tile_pool(name="work", bufs=3))
        banks = ctx.enter_context(tc.psum_pool(name="banks", bufs=4))
        halves = ctx.enter_context(tc.psum_pool(name="halves", bufs=1))
        accs = ctx.enter_context(tc.psum_pool(name="accs", bufs=2))
        ctx.enter_context(tc.manual_schedule())

        t0row = const.tile([P, ROWS], BF16, name="t0row")
        nc.vector.memset(t0row[:], 0.0)
        ones = const.tile([P, P], BF16, name="ones")
        nc.vector.memset(ones[:], 1.0)
        ident = const.tile([P, P], F32, name="ident")
        make_identity(nc, ident[:])
        zero = const.tile([P, P], F32, name="zero")
        nc.vector.memset(zero[:], 0.0)
        t0b = const.tile([P, ROWS], BF16, name="t0b")
        minus_half = const.tile([P, P], BF16, name="minus_half")
        nc.vector.memset(minus_half[:], -0.5)

        wm = {}
        for t in range(2):
            for parity in range(2):
                wm[(t, parity)] = const.tile([P, CHUNKS * CHUNK], BF16, name="wm_%d_%d" % (t, parity))
                if parity == 0:
                    nc.vector.memset(wm[(t, parity)][:, WIN:], 0.0)
                else:
                    nc.vector.memset(wm[(t, parity)][:, 0 : CHUNKS * CHUNK - WIN], 0.0)

        zg = const.tile([P, PASSES, 4 * BATCH], BF16, name="zg", align_bytes=64)
        z_codes = const.tile([P, PASSES, BATCH], U32, name="z_codes", align_bytes=64)
        z_scales = const.tile([P, PASSES, BATCH], U8, name="z_scales", align_bytes=64)
        x1_sb = const.tile([P, M_TILES, ROWS], F32, name="x1_sb")
        x2_sb = const.tile([P, M_TILES, ROWS], F32, name="x2_sb")

        z_sb = {}
        mk_sb = [loads.tile([P, WIN], BF16, name="mk_sb%d" % g) for g in range(GROUPS)]
        t_sb = [[loads.tile([P, WIN], BF16, name="t%d_sb%d" % (t, g)) for g in range(GROUPS)] for t in range(2)]
        new_passes = []
        have = 0
        for g in range(GROUPS):
            y0, chunk0, margin, first_pass, last_pass = group_geometry(g)
            new_passes.append(list(range(have, last_pass + 1)))
            for dst, src in ((mk_sb[g], mask), (t_sb[0][g], T1), (t_sb[1][g], T2)):
                rows = src.rearrange("(s g j) k -> g j s k", s=STACK, g=GROUPS)
                nc.sync.dma_start(out=dst[:], in_=rows[g, :, :, IMG * y0 : IMG * y0 + WIN])
                if g == 0 and src is mask:
                    nc.sync.dma_start(out=t0row[0:1, :], in_=T0.rearrange("(o r) -> o r", o=1))
            if last_pass + 1 > have:
                z_part = loads.tile([P, M_TILES, K_PASS * (last_pass + 1 - have)], BF16, name="z_part%d" % g)
                nc.sync.dma_start(
                    out=z_part[:],
                    in_=z.rearrange("(m p) k -> p m k", p=P)[:, :, K_PASS * have : K_PASS * (last_pass + 1)],
                )
                for c in range(have, last_pass + 1):
                    z_sb[c] = (z_part, K_PASS * (c - have))
                have = last_pass + 1

        warm = const.tile([P, 1], F32, name="warm")
        nc.scalar.copy(out=warm[:], in_=zero[:, 0:1])

        def spread_t0():
            bank = banks.tile([P, ROWS], BF16, name="t0_bank", tag="bank")
            for h in range(2):
                cols = slice(512 * h, 512 * (h + 1))
                nc.tensor.matmul(out=bank[:, cols], lhsT=ones[:], rhs=t0row[:, cols], start=True, stop=True)
            nc.scalar.copy(out=t0b[:], in_=bank[:])

        def quarter(bank, split, t, u):
            if split:
                return bank[:].rearrange("p (b t u r) -> p t u b r", b=2, t=2, u=2)[:, t, u]
            return bank[:].rearrange("p (t u n) -> p t u n", t=2, u=2)[:, t, u]

        half_bank = []
        for u_zero in range(2):
            bank = halves.tile([P, 4 * P], F32, name="half_bank%d" % u_zero)
            for t in range(2):
                nc.tensor.transpose(quarter(bank, True, t, u_zero), zero[:], ident[:])
            half_bank.append(bank)

        def z_prepare(c):
            bank = banks.tile([P, 4 * P], F32, name="bank", tag="bank")
            z_part, k0 = z_sb[c]
            for m in range(M_TILES):
                words = z_part[:, m, :].bitcast(F32)
                for u in range(2):
                    w0 = k0 // 2 + u * P
                    q = 2 * m + u
                    nc.tensor.transpose(bank[:, P * q : P * (q + 1)], words[:, w0 : w0 + P], ident[:])
            nc.scalar.copy(
                out=zg[:, c, :].bitcast(F32).rearrange("p (m b u) -> p m b u", m=M_TILES, u=2),
                in_=bank[:].rearrange("p (m u b) -> p m b u", m=M_TILES, u=2),
            )

        def z_quantise(c):
            nc.vector.quantize_mx(out=z_codes[:, c, :].bitcast(FP8X4), scales=z_scales[:, c, :], in_=zg[:, c, :])

        state = {}

        def products(g):
            margin = group_geometry(g)[2]
            for t in range(2):
                nc.vector.tensor_tensor(
                    out=wm[(t, g % 2)][:, margin : margin + WIN], in0=t_sb[t][g][:], in1=mk_sb[g][:], op=MULT
                )

        def spread_weights(g):
            y0, chunk0, margin, first_pass, last_pass = group_geometry(g)
            both, single = pass_order(g)
            split = len(single) > 0
            wg = work.tile([P, 4 * 4 * 2 * P], BF16, name="wg", tag="wg", align_bytes=64)
            for c in range(first_pass, last_pass + 1):
                inside = [u for u in range(2) if 0 <= 2 * c + u - chunk0 < CHUNKS]
                if len(inside) == 2:
                    bank = banks.tile([P, 4 * P], F32, name="bank", tag="bank")
                else:
                    bank = half_bank[1 - inside[0]]
                for t in range(2):
                    words = wm[(t, g % 2)][:].bitcast(F32)
                    for u in inside:
                        ch = 2 * c + u - chunk0
                        nc.tensor.transpose(quarter(bank, split, t, u), words[:, P * ch : P * (ch + 1)], ident[:])
                if c in both:
                    src, at = bank[:], 4 * P * both.index(c)
                else:
                    b = 0 if needed(g, c, 0) else 1
                    src, at = bank[:, 2 * P * b : 2 * P * (b + 1)], 4 * P * len(both)
                n = src.shape[1]
                r = P // 2 if split else P
                copy = nc.vector.tensor_copy if g == 0 and c == 1 else nc.scalar.copy
                copy(
                    out=wg[:].bitcast(F32)[:, at : at + n].rearrange("p (q r u) -> p q r u", r=r, u=2),
                    in_=src.rearrange("p (q u r) -> p q r u", r=r, u=2),
                )
            state[g] = wg

        def w_quantise(g):
            both, single = pass_order(g)
            wg = state[g]
            w_codes = work.tile([P, 4 * 2 * P], U32, name="w_codes", tag="w_codes", align_bytes=64)
            w_scales = work.tile([P, 4 * 2 * P], U8, name="w_scales", tag="w_scales", align_bytes=64)
            a = 0
            for n in [4 * P, 2 * P] + [P] * len(single):
                nc.vector.quantize_mx(
                    out=w_codes[:, a : a + n].bitcast(FP8X4), scales=w_scales[:, a : a + n], in_=wg[:, 4 * a : 4 * (a + n)]
                )
                a += n
            state[g] = (w_codes, w_scales)

        def multiply(g):
            both, single = pass_order(g)
            w_codes, w_scales = state[g]
            acc = accs.tile([P, M_TILES, 2 * P], F32, name="acc", tag="acc")
            for m in range(M_TILES):
                groups = [(0, 2 * P, [(c, 2 * P * i) for i, c in enumerate(both)])]
                if single:
                    groups = []
                    for b in range(2):
                        terms = [(c, 2 * P * i + P * b) for i, c in enumerate(both)]
                        terms += [(c, 2 * P * len(both)) for c in single if needed(g, c, b)]
                        groups.append((P * b, P, terms))
                for n0, n, terms in groups:
                    for i, (c, a) in enumerate(terms):
                        nc.tensor.matmul_mx(
                            out=acc[:, m, n0 : n0 + n],
                            lhsT=z_codes[:, c, P * m : P * (m + 1)].bitcast(FP8X4),
                            lhsT_scale=z_scales[:, c, P * m : P * (m + 1)],
                            rhs=w_codes[:, a : a + n].bitcast(FP8X4),
                            rhs_scale=w_scales[:, a : a + n],
                            start=(i == 0),
                            stop=(i == len(terms) - 1),
                        )
            state[g] = acc

        def views(g):
            x1_v = x1_sb[:].rearrange("p m (s g j) -> p m s g j", s=STACK, g=GROUPS)[:, :, :, g, :]
            x2_v = x2_sb[:].rearrange("p m (s g j) -> p m s g j", s=STACK, g=GROUPS)[:, :, :, g, :]
            if not pass_order(g)[1]:
                acc_v = state[g][:].rearrange("p m (t j s) -> p m t s j", t=2, s=STACK)
                return [(acc_v, x1_v, x2_v)]
            acc_v = state[g][:].rearrange("p m (b t x s) -> p b m t s x", b=2, t=2, s=STACK)
            return [(acc_v[:, b], x1_v[:, :, :, POS * b : POS * (b + 1)], x2_v[:, :, :, POS * b : POS * (b + 1)]) for b in range(2)]

        def x1_out(g, ms):
            for acc_v, x1_v, x2_v in views(g):
                nc.scalar.copy(out=x1_v[:, ms], in_=acc_v[:, ms, 0])

        def x2_product(g, ms):
            for acc_v, x1_v, x2_v in views(g):
                nc.vector.tensor_tensor(out=x2_v[:, ms], in0=acc_v[:, ms, 1], in1=x1_v[:, ms], op=MULT)

        half_x2 = {}

        def half_x2_product(g):
            prod = work.tile([P, M_TILES, P], F32, name="prod", tag="prod")
            if pass_order(g)[1]:
                x1_v = x1_sb[:].rearrange("p m (s g b x) -> p b m g x s", s=STACK, g=GROUPS, b=2)
                acc_v = state[g][:].rearrange("p m (b t x s) -> p b m t x s", b=2, t=2, s=STACK)
                out_v = prod[:].rearrange("p m (b x s) -> p b m x s", b=2, s=STACK)
                pieces = [(out_v[:, b], acc_v[:, b, :, 1], x1_v[:, b, :, g]) for b in range(2)]
            else:
                x1_v = x1_sb[:].rearrange("p m (s g j) -> p m g j s", s=STACK, g=GROUPS)
                acc_v = state[g][:].rearrange("p m (t j s) -> p m t j s", t=2, s=STACK)
                pieces = [(prod[:].rearrange("p m (j s) -> p m j s", s=STACK), acc_v[:, :, 1], x1_v[:, :, g])]
            for out, in0, in1 in pieces:
                nc.vector.tensor_tensor(out=out, in0=in0, in1=in1, op=MULT)
            half_x2[g] = prod

        def half_x2_sum(g):
            bank = banks.tile([P, 4 * P], F32, name="x2_bank", tag="bank")
            t0_g = t0row[:].rearrange("p (s g j) -> p g j s", s=STACK, g=GROUPS)[:, g]
            both_m = bank[:, 0 : M_TILES * P]
            t0_m = t0_g.unsqueeze(1).to_broadcast([P, M_TILES, J, STACK])
            nc.tensor.matmul(out=both_m, lhsT=minus_half[:], rhs=t0_m, start=True, stop=False)
            nc.tensor.matmul(
                out=both_m, lhsT=ident[:], rhs=half_x2[g][:].rearrange("p m n -> p (m n)"), start=False, stop=True
            )
            half_x2[g] = bank

        def x2_out(g):
            nc.scalar.mul(
                out=x2_sb[:].rearrange("p m (s g j) -> p m s g j", s=STACK, g=GROUPS)[:, :, :, g, :],
                in_=half_x2[g][:, 0 : M_TILES * P].rearrange("p (m j s) -> p m s j", m=M_TILES, s=STACK),
                mul=2.0,
            )

        def store(sb, dram, ga, gb, m):
            nc.sync.dma_start(
                out=dram[P * m : P * (m + 1), :].rearrange("p (s c) -> p s c", s=STACK)[:, :, J * ga : J * gb],
                in_=sb[:, m, :].rearrange("p (s c) -> p s c", s=STACK)[:, :, J * ga : J * gb],
            )

        def x2_finish(ga, gb):
            t0_r = t0b[:].rearrange("p (s c) -> p s c", s=STACK)[:, :, J * ga : J * gb]
            for m in range(M_TILES):
                x2_r = x2_sb[:, m, :].rearrange("p (s c) -> p s c", s=STACK)[:, :, J * ga : J * gb]
                nc.vector.scalar_tensor_tensor(out=x2_r, in0=x2_r, scalar=2.0, in1=t0_r, op0=MULT, op1=SUBTRACT)
                store(x2_sb, out_1, ga, gb, m)

        store_after = {3: (0, 4), 5: (4, 6), 7: (6, 8)}
        spread_t0()
        for step in range(GROUPS + 2):
            done = step - 2
            if done >= 0:
                pieces = [slice(0, M_TILES)] if done < GROUPS - 1 else [slice(m, m + 1) for m in range(M_TILES)]
                for ms in pieces:
                    x1_out(done, ms)
                if done in store_after:
                    for m in range(M_TILES):
                        store(x1_sb, out_0, *store_after[done], m)
            if step == 0:
                products(0)
                spread_weights(0)
                for c in new_passes[0]:
                    z_prepare(c)
            elif step < GROUPS:
                if step == 1:
                    w_quantise(0)
                for c in new_passes[step]:
                    z_prepare(c)
                if 0 <= done - 1 < OFFLOADED:
                    half_x2_sum(done - 1)
                    x2_out(done - 1)
                    if done == OFFLOADED:
                        for m in range(M_TILES):
                            store(x2_sb, out_1, 0, OFFLOADED, m)
                products(step)
                spread_weights(step)
            if step < GROUPS and done > OFFLOADED and done - 1 in store_after:
                x2_finish(*store_after[done - 1])
            if 1 <= step <= GROUPS:
                if step > 1:
                    w_quantise(step - 1)
                for c in new_passes[step - 1]:
                    z_quantise(c)
                multiply(step - 1)
            if step >= GROUPS and done - 1 in store_after:
                x2_finish(*store_after[done - 1])
            if done >= 0:
                if done < OFFLOADED:
                    half_x2_product(done)
                elif done < GROUPS - 1:
                    x2_product(done, slice(0, M_TILES))
                else:
                    for m in range(M_TILES):
                        x2_product(done, slice(m, m + 1))
                    x2_finish(*store_after[done])
